import numpy as np
import ml_dtypes


def mxq(x, axis, fmt="e4m3"):
    dtype, down = {"e4m3": (ml_dtypes.float8_e4m3fn, 7), "e5m2": (ml_dtypes.float8_e5m2, 14)}[fmt]
    v = np.moveaxis(np.asarray(x, np.float32).astype(ml_dtypes.bfloat16).astype(np.float64), axis, -1)
    blocks = v.reshape(v.shape[:-1] + (-1, 32))
    amax = np.abs(blocks).max(-1, keepdims=True)
    byte = np.maximum(np.where(amax > 0, np.frexp(amax)[1] - 1 + 127, 0) - down, 1)
    scale = np.exp2(byte - 127.0)
    codes = (blocks / scale).astype(np.float32).astype(dtype).astype(np.float64)
    return np.moveaxis((codes * scale).reshape(v.shape), -1, axis)


WIDE = False


def mx_kscale(k):
    if not WIDE:
        return np.ones(k)
    levels = np.array([10, -10, 5, -5, 0])
    a = np.random.permutation(np.resize(levels, k // 512 * 4)).reshape(k // 512, 4)
    idx = np.arange(k)
    return np.exp2(a[idx // 512, idx % 128 // 32])


BF16 = ml_dtypes.bfloat16


def bf(x):
    return np.asarray(x, np.float32).astype(BF16)


def f64(x):
    return np.asarray(x).astype(np.float64)


B, H, S, D = 4, 4, 1024, 128
TEMPERATURE = 8.0
QK = np.sqrt(1.5 * TEMPERATURE / np.sqrt(D))
VS = 3.0


def setup_inputs():
    t = mx_kscale(S)
    a = np.log2(t / t.min())
    q = np.random.standard_normal((B, H, S, D)) * QK
    k = np.random.standard_normal((B, H, S, D)) * QK
    v = np.random.standard_normal((B, H, S, D)) * VS
    q[..., 0] = TEMPERATURE
    k[..., 0] += a * np.log(2.0)
    v = v * (t.max() / t)[:, None]
    return {"q": bf(q), "k": bf(k), "v": bf(v),
            "mask": bf(np.random.randint(0, 2, (1, 1, S, S)))}


def reference(q, k, v, mask):
    s = f64(q) @ f64(k).transpose(0, 1, 3, 2) / TEMPERATURE * f64(mask)
    e = np.exp(s - s.max(-1, keepdims=True))
    return (mxq(e, 3, "e4m3") @ mxq(f64(v), 2, "e4m3")) / e.sum(-1, keepdims=True)

@@ -1,0 +1,252 @@
+from contextlib import ExitStack
+
+import concourse.mybir as mybir
+from concourse.masks import make_identity
+
+BF16 = mybir.dt.bfloat16
+F32 = mybir.dt.float32
+U32 = mybir.dt.uint32
+U8 = mybir.dt.uint8
+FP8X4 = mybir.dt.float8_e4m3fn_x4
+ALU = mybir.AluOpType
+ACT = mybir.ActivationFunctionType
+
+P = 128
+HEADS = 16
+S = 1024
+D = 128
+TEMPERATURE = 8.0
+Q_TILES = S // P
+UNITS = HEADS * Q_TILES
+BANK = 512
+HALVES = S // BANK
+PACK = 4
+K_PASS = P * PACK
+PASSES = S // K_PASS
+PAIR = 2
+WORD_BLOCKS = S // (PAIR * P)
+
+FLOPS = 2 * 2 * HEADS * S * S * D
+
+LOAD_LEAD = 18
+MASK_LEAD = 17
+QK_T_LEAD = 10
+V_LEAD = 2
+SCORE_LEAD = 1
+EXP_LAG = 1
+E_T_LAG = 2
+PV_LAG = 3
+
+
+def tile_scaleddotproductattention_pa_kernel(tc, q, k, v, mask, out):
+    nc = tc.nc
+
+    q_heads = q.rearrange("b h (p t) d -> (b h) p t d", t=Q_TILES)
+    k_heads = k.rearrange("b h (t p) d -> (b h) p t d", p=P)
+    mask_tiles = mask.rearrange("a b (p t) k -> (a b) p t k", t=Q_TILES)
+    out_heads = out.rearrange("b h (p t) d -> (b h) p t d", t=Q_TILES)
+    v_heads = v.rearrange("b h (c p e) d -> (b h) p c (e d)", p=P, e=PAIR)
+
+    with ExitStack() as ctx:
+        consts = ctx.enter_context(tc.tile_pool(name="consts", bufs=1))
+        loads = ctx.enter_context(tc.tile_pool(name="loads", bufs=3))
+        heads = ctx.enter_context(tc.tile_pool(name="heads", bufs=3))
+        work = ctx.enter_context(tc.tile_pool(name="work", bufs=3))
+        small = ctx.enter_context(tc.tile_pool(name="small", bufs=6))
+        score_psum = ctx.enter_context(tc.psum_pool(name="score_psum", bufs=2 * HALVES))
+        e_t_psum = ctx.enter_context(tc.psum_pool(name="e_t_psum", bufs=2))
+        qk_t_psum = ctx.enter_context(tc.psum_pool(name="qk_t_psum", bufs=1))
+        out_psum = ctx.enter_context(tc.psum_pool(name="out_psum", bufs=1))
+
+        ident_bf16 = consts.tile([P, P], BF16)
+        make_identity(nc, ident_bf16[:])
+        ident_f32 = consts.tile([P, P], F32)
+        make_identity(nc, ident_f32[:])
+        mask_sb = consts.tile([P, Q_TILES, S], BF16)
+
+        q_rows, k_rows, v_rows = {}, {}, {}
+        qk_t, v_codes, v_scales, out_rows = {}, {}, {}, {}
+        scores, masked, neg_max, e_rows, row_sum = {}, {}, {}, {}, {}
+        e_t, e_grouped, e_codes, e_scales, pv = {}, {}, {}, {}, {}
+
+        def load_head(head):
+            q_in = loads.tile([P, Q_TILES, D], BF16)
+            nc.sync.dma_start(out=q_in[:], in_=q_heads[head])
+            k_in = loads.tile([P, Q_TILES, D], BF16)
+            nc.sync.dma_start(out=k_in[:], in_=k_heads[head])
+            v_in = loads.tile([P, PASSES, PACK, D], BF16)
+            nc.sync.dma_start(
+                out=v_in[:].rearrange("p g (u e) d -> p (g u) (e d)", e=PAIR), in_=v_heads[head]
+            )
+            q_rows[head], k_rows[head], v_rows[head] = q_in, k_in, v_in
+
+        def transpose_q_and_k(unit):
+            head, tile_index = divmod(unit, Q_TILES)
+            if tile_index == 0:
+                qk_cols = heads.tile([P, 2, Q_TILES, P], BF16)
+                qk_t[head] = qk_cols
+            qk_bank = qk_t_psum.tile([P, 2, P], BF16)
+            nc.tensor.transpose(qk_bank[:, 0, :], q_rows[head][:, tile_index, :], ident_bf16[:])
+            nc.tensor.transpose(qk_bank[:, 1, :], k_rows[head][:, tile_index, :], ident_bf16[:])
+            nc.scalar.copy(out=qk_t[head][:, :, tile_index, :], in_=qk_bank[:])
+
+        def quantise_v(head):
+            v_grouped = heads.tile([P, PASSES, D, PACK], BF16, align_bytes=64)
+            nc.vector.tensor_copy(
+                out=v_grouped[:], in_=v_rows[head][:].rearrange("p g t d -> p g d t")
+            )
+            codes = heads.tile([P, PASSES, D], U32, align_bytes=64, name="v_code_words")
+            scale_plane = heads.tile([P, PASSES, D], U8, align_bytes=64, name="v_scale_plane")
+            nc.vector.quantize_mx(
+                out=codes[:].rearrange("p g d -> p (g d)").bitcast(FP8X4),
+                scales=scale_plane[:].rearrange("p g d -> p (g d)"),
+                in_=v_grouped[:].rearrange("p g d t -> p (g d t)"),
+            )
+            v_codes[head], v_scales[head] = codes, scale_plane
+
+        def multiply_q_k(unit):
+            head, tile_index = divmod(unit, Q_TILES)
+            for half in range(HALVES):
+                score_bank = score_psum.tile([P, BANK], F32)
+                key_tiles = slice(half * BANK // P, (half + 1) * BANK // P)
+                nc.tensor.matmul(
+                    out=score_bank[:],
+                    lhsT=qk_t[head][:, 0, tile_index, :],
+                    rhs=qk_t[head][:, 1, key_tiles, :].rearrange("d t p -> d (t p)"),
+                    start=True,
+                    stop=True,
+                )
+                scores[unit, half] = score_bank
+
+        def mask_scores(unit):
+            tile_index = unit % Q_TILES
+            masked_rows = work.tile([P, S], F32)
+            for half in range(HALVES):
+                keys = slice(half * BANK, (half + 1) * BANK)
+                nc.vector.scalar_tensor_tensor(
+                    out=masked_rows[:, keys],
+                    in0=scores[unit, half][:],
+                    scalar=1.0 / TEMPERATURE,
+                    in1=mask_sb[:, tile_index, keys],
+                    op0=ALU.mult,
+                    op1=ALU.mult,
+                )
+            masked[unit] = masked_rows
+
+        def row_maximum(unit):
+            minus_max = small.tile([P, 1], F32)
+            nc.vector.tensor_reduce(
+                out=minus_max[:],
+                in_=masked[unit][:],
+                axis=mybir.AxisListType.X,
+                op=ALU.max,
+                negate=True,
+            )
+            neg_max[unit] = minus_max
+
+        def exponentials(unit):
+            e_bf16 = work.tile([P, S], BF16)
+            e_sum = small.tile([P, 1], F32)
+            nc.scalar.activation(
+                out=e_bf16[:],
+                in_=masked[unit][:],
+                func=ACT.Exp,
+                bias=neg_max[unit][:],
+                scale=1.0,
+                accum_out=e_sum[:],
+            )
+            e_rows[unit], row_sum[unit] = e_bf16, e_sum
+
+        def transpose_e(unit):
+            e_words = e_rows[unit][:].bitcast(F32)
+            e_words_t = e_t_psum.tile([P, WORD_BLOCKS, P], F32)
+            for c in range(WORD_BLOCKS):
+                nc.tensor.transpose(
+                    e_words_t[:, c, :], e_words[:, c * P : (c + 1) * P], ident_f32[:]
+                )
+            e_t[unit] = e_words_t
+
+        def regroup_e(unit):
+            grouped = work.tile([P, PASSES, P, PACK], BF16, align_bytes=64)
+            nc.scalar.copy(
+                out=grouped[:].bitcast(F32),
+                in_=e_t[unit][:].rearrange("p (g u) n -> p g n u", u=PAIR),
+            )
+            e_grouped[unit] = grouped
+
+        def quantise_e(unit):
+            codes = work.tile([P, PASSES, P], U32, align_bytes=64, name="e_code_words")
+            scale_plane = work.tile([P, PASSES, P], U8, align_bytes=64, name="e_scale_plane")
+            nc.vector.quantize_mx(
+                out=codes[:].rearrange("p g n -> p (g n)").bitcast(FP8X4),
+                scales=scale_plane[:].rearrange("p g n -> p (g n)"),
+                in_=e_grouped[unit][:].rearrange("p g n t -> p (g n t)"),
+            )
+            e_codes[unit], e_scales[unit] = codes, scale_plane
+
+        def multiply_e_v(unit):
+            head = unit // Q_TILES
+            pv_bank = out_psum.tile([P, D], F32)
+            for g in range(PASSES):
+                nc.tensor.matmul_mx(
+                    out=pv_bank[:],
+                    lhsT=e_codes[unit][:, g, :].bitcast(FP8X4),
+                    lhsT_scale=e_scales[unit][:, g, :],
+                    rhs=v_codes[head][:, g, :].bitcast(FP8X4),
+                    rhs_scale=v_scales[head][:, g, :],
+                    start=(g == 0),
+                    stop=(g == PASSES - 1),
+                )
+            pv[unit] = pv_bank
+
+        def invert_row_sum(unit):
+            inverse = small.tile([P, 1], F32)
+            nc.vector.reciprocal(out=inverse[:], in_=row_sum[unit][:])
+            row_sum[unit] = inverse
+
+        def divide_and_store(unit):
+            head, tile_index = divmod(unit, Q_TILES)
+            if tile_index == 0:
+                out_sb = heads.tile([P, Q_TILES, D], F32)
+                out_rows[head] = out_sb
+            nc.scalar.activation(
+                out=out_rows[head][:, tile_index, :],
+                in_=pv[unit][:],
+                func=ACT.Copy,
+                scale=row_sum[unit][:],
+            )
+            if tile_index == Q_TILES - 1:
+                nc.sync.dma_start(out=out_heads[head], in_=out_rows[head][:])
+
+        def is_unit(index):
+            return 0 <= index < UNITS
+
+        ctx.enter_context(tc.manual_schedule())
+        for step in range(-LOAD_LEAD, UNITS + PV_LAG):
+            if is_unit(step + LOAD_LEAD) and (step + LOAD_LEAD) % Q_TILES == 0:
+                load_head((step + LOAD_LEAD) // Q_TILES)
+            if 0 <= step + MASK_LEAD < Q_TILES:
+                tile_index = step + MASK_LEAD
+                nc.sync.dma_start(out=mask_sb[:, tile_index, :], in_=mask_tiles[0, :, tile_index, :])
+            if is_unit(step - E_T_LAG):
+                transpose_e(step - E_T_LAG)
+            if is_unit(step + SCORE_LEAD):
+                multiply_q_k(step + SCORE_LEAD)
+            if is_unit(step):
+                mask_scores(step)
+            if is_unit(step - EXP_LAG):
+                exponentials(step - EXP_LAG)
+            if is_unit(step - PV_LAG):
+                invert_row_sum(step - PV_LAG)
+                quantise_e(step - PV_LAG)
+                multiply_e_v(step - PV_LAG)
+            if is_unit(step - E_T_LAG):
+                regroup_e(step - E_T_LAG)
+            if is_unit(step):
+                row_maximum(step)
+            if is_unit(step - PV_LAG):
+                divide_and_store(step - PV_LAG)
+            if is_unit(step + V_LEAD) and (step + V_LEAD) % Q_TILES == 0:
+                quantise_v((step + V_LEAD) // Q_TILES)
+            if is_unit(step + QK_T_LEAD):
+                transpose_q_and_k(step + QK_T_LEAD)

@@ -32,10 +32,13 @@ LOAD_LEAD = 18
 MASK_LEAD = 17
 QK_T_LEAD = 10
 V_LEAD = 2
-SCORE_LEAD = 1
+SCORE_LEAD = 2
+DETOUR_LEAD = 1
 EXP_LAG = 1
 E_T_LAG = 2
 PV_LAG = 3
+
+DETOUR_EVERY = 3
 
 
 def tile_scaleddotproductattention_pa_kernel(tc, q, k, v, mask, out):
@@ -51,7 +54,7 @@ def tile_scaleddotproductattention_pa_kernel(tc, q, k, v, mask, out):
         consts = ctx.enter_context(tc.tile_pool(name="consts", bufs=1))
         loads = ctx.enter_context(tc.tile_pool(name="loads", bufs=3))
         heads = ctx.enter_context(tc.tile_pool(name="heads", bufs=3))
-        work = ctx.enter_context(tc.tile_pool(name="work", bufs=3))
+        work = ctx.enter_context(tc.tile_pool(name="work", bufs=4))
         small = ctx.enter_context(tc.tile_pool(name="small", bufs=6))
         score_psum = ctx.enter_context(tc.psum_pool(name="score_psum", bufs=2 * HALVES))
         e_t_psum = ctx.enter_context(tc.psum_pool(name="e_t_psum", bufs=2))
@@ -104,8 +107,13 @@ def tile_scaleddotproductattention_pa_kernel(tc, q, k, v, mask, out):
             )
             v_codes[head], v_scales[head] = codes, scale_plane
 
+        def takes_detour(unit, half):
+            return unit % DETOUR_EVERY == DETOUR_EVERY - 1 and half == HALVES - 1
+
         def multiply_q_k(unit):
             head, tile_index = divmod(unit, Q_TILES)
+            masked_rows = work.tile([P, S], F32)
+            masked[unit] = masked_rows
             for half in range(HALVES):
                 score_bank = score_psum.tile([P, BANK], F32)
                 key_tiles = slice(half * BANK // P, (half + 1) * BANK // P)
@@ -120,18 +128,31 @@ def tile_scaleddotproductattention_pa_kernel(tc, q, k, v, mask, out):
 
         def mask_scores(unit):
             tile_index = unit % Q_TILES
-            masked_rows = work.tile([P, S], F32)
             for half in range(HALVES):
                 keys = slice(half * BANK, (half + 1) * BANK)
-                nc.vector.scalar_tensor_tensor(
-                    out=masked_rows[:, keys],
-                    in0=scores[unit, half][:],
-                    scalar=1.0 / TEMPERATURE,
-                    in1=mask_sb[:, tile_index, keys],
-                    op0=ALU.mult,
-                    op1=ALU.mult,
-                )
-            masked[unit] = masked_rows
+                if not takes_detour(unit, half):
+                    nc.vector.scalar_tensor_tensor(
+                        out=masked[unit][:, keys],
+                        in0=scores[unit, half][:],
+                        scalar=1.0 / TEMPERATURE,
+                        in1=mask_sb[:, tile_index, keys],
+                        op0=ALU.mult,
+                        op1=ALU.mult,
+                    )
+
+        def mask_scores_on_detour(unit):
+            tile_index = unit % Q_TILES
+            for half in range(HALVES):
+                keys = slice(half * BANK, (half + 1) * BANK)
+                if takes_detour(unit, half):
+                    scaled = work.tile([P, BANK], F32)
+                    nc.scalar.mul(out=scaled[:], in_=scores[unit, half][:], mul=1.0 / TEMPERATURE)
+                    nc.gpsimd.tensor_tensor(
+                        out=masked[unit][:, keys],
+                        in0=scaled[:],
+                        in1=mask_sb[:, tile_index, keys],
+                        op=ALU.mult,
+                    )
 
         def row_maximum(unit):
             minus_max = small.tile([P, 1], F32)
@@ -230,12 +251,14 @@ def tile_scaleddotproductattention_pa_kernel(tc, q, k, v, mask, out):
                 nc.sync.dma_start(out=mask_sb[:, tile_index, :], in_=mask_tiles[0, :, tile_index, :])
             if is_unit(step - E_T_LAG):
                 transpose_e(step - E_T_LAG)
-            if is_unit(step + SCORE_LEAD):
-                multiply_q_k(step + SCORE_LEAD)
             if is_unit(step):
                 mask_scores(step)
+            if is_unit(step + SCORE_LEAD):
+                multiply_q_k(step + SCORE_LEAD)
             if is_unit(step - EXP_LAG):
                 exponentials(step - EXP_LAG)
+            if is_unit(step + DETOUR_LEAD):
+                mask_scores_on_detour(step + DETOUR_LEAD)
             if is_unit(step - PV_LAG):
                 invert_row_sum(step - PV_LAG)
                 quantise_e(step - PV_LAG)

@@ -18,8 +18,10 @@ D = 128
 TEMPERATURE = 8.0
 Q_TILES = S // P
 UNITS = HEADS * Q_TILES
+GROUP = 4
 BANK = 512
 HALVES = S // BANK
+FIRST_HALF, LAST_HALF = 0, HALVES - 1
 PACK = 4
 K_PASS = P * PACK
 PASSES = S // K_PASS
@@ -31,14 +33,15 @@ FLOPS = 2 * 2 * HEADS * S * S * D
 LOAD_LEAD = 18
 MASK_LEAD = 17
 QK_T_LEAD = 10
-V_LEAD = 2
+V_LEAD = 3
 SCORE_LEAD = 2
 DETOUR_LEAD = 1
 EXP_LAG = 1
 E_T_LAG = 2
-PV_LAG = 3
+PV_LAG = 4
+OUT_LAG = 5
 
-DETOUR_EVERY = 3
+DETOUR_EVERY = 2
 
 
 def tile_scaleddotproductattention_pa_kernel(tc, q, k, v, mask, out):
@@ -55,7 +58,7 @@ def tile_scaleddotproductattention_pa_kernel(tc, q, k, v, mask, out):
         loads = ctx.enter_context(tc.tile_pool(name="loads", bufs=3))
         heads = ctx.enter_context(tc.tile_pool(name="heads", bufs=3))
         work = ctx.enter_context(tc.tile_pool(name="work", bufs=4))
-        small = ctx.enter_context(tc.tile_pool(name="small", bufs=6))
+        groups = ctx.enter_context(tc.tile_pool(name="groups", bufs=3))
         score_psum = ctx.enter_context(tc.psum_pool(name="score_psum", bufs=2 * HALVES))
         e_t_psum = ctx.enter_context(tc.psum_pool(name="e_t_psum", bufs=2))
         qk_t_psum = ctx.enter_context(tc.psum_pool(name="qk_t_psum", bufs=1))
@@ -69,8 +72,8 @@ def tile_scaleddotproductattention_pa_kernel(tc, q, k, v, mask, out):
 
         q_rows, k_rows, v_rows = {}, {}, {}
         qk_t, v_codes, v_scales, out_rows = {}, {}, {}, {}
-        scores, masked, neg_max, e_rows, row_sum = {}, {}, {}, {}, {}
-        e_t, e_grouped, e_codes, e_scales, pv = {}, {}, {}, {}, {}
+        e_grouped, row_sums, pv = {}, {}, {}
+        scores, masked, neg_max, e_rows, e_t = {}, {}, {}, {}, {}
 
         def load_head(head):
             q_in = loads.tile([P, Q_TILES, D], BF16)
@@ -107,8 +110,8 @@ def tile_scaleddotproductattention_pa_kernel(tc, q, k, v, mask, out):
             )
             v_codes[head], v_scales[head] = codes, scale_plane
 
-        def takes_detour(unit, half):
-            return unit % DETOUR_EVERY == DETOUR_EVERY - 1 and half == HALVES - 1
+        def takes_detour(unit):
+            return unit % DETOUR_EVERY == 0
 
         def multiply_q_k(unit):
             head, tile_index = divmod(unit, Q_TILES)
@@ -126,36 +129,30 @@ def tile_scaleddotproductattention_pa_kernel(tc, q, k, v, mask, out):
                 )
                 scores[unit, half] = score_bank
 
-        def mask_scores(unit):
-            tile_index = unit % Q_TILES
-            for half in range(HALVES):
-                keys = slice(half * BANK, (half + 1) * BANK)
-                if not takes_detour(unit, half):
-                    nc.vector.scalar_tensor_tensor(
-                        out=masked[unit][:, keys],
-                        in0=scores[unit, half][:],
-                        scalar=1.0 / TEMPERATURE,
-                        in1=mask_sb[:, tile_index, keys],
-                        op0=ALU.mult,
-                        op1=ALU.mult,
-                    )
+        def mask_scores(unit, half):
+            keys = slice(half * BANK, (half + 1) * BANK)
+            nc.vector.scalar_tensor_tensor(
+                out=masked[unit][:, keys],
+                in0=scores[unit, half][:],
+                scalar=1.0 / TEMPERATURE,
+                in1=mask_sb[:, unit % Q_TILES, keys],
+                op0=ALU.mult,
+                op1=ALU.mult,
+            )
 
-        def mask_scores_on_detour(unit):
-            tile_index = unit % Q_TILES
-            for half in range(HALVES):
-                keys = slice(half * BANK, (half + 1) * BANK)
-                if takes_detour(unit, half):
-                    scaled = work.tile([P, BANK], F32)
-                    nc.scalar.mul(out=scaled[:], in_=scores[unit, half][:], mul=1.0 / TEMPERATURE)
-                    nc.gpsimd.tensor_tensor(
-                        out=masked[unit][:, keys],
-                        in0=scaled[:],
-                        in1=mask_sb[:, tile_index, keys],
-                        op=ALU.mult,
-                    )
+        def mask_scores_on_detour(unit, half):
+            keys = slice(half * BANK, (half + 1) * BANK)
+            scaled = work.tile([P, BANK], F32)
+            nc.scalar.mul(out=scaled[:], in_=scores[unit, half][:], mul=1.0 / TEMPERATURE)
+            nc.gpsimd.tensor_tensor(
+                out=masked[unit][:, keys],
+                in0=scaled[:],
+                in1=mask_sb[:, unit % Q_TILES, keys],
+                op=ALU.mult,
+            )
 
         def row_maximum(unit):
-            minus_max = small.tile([P, 1], F32)
+            minus_max = work.tile([P, 1], F32)
             nc.vector.tensor_reduce(
                 out=minus_max[:],
                 in_=masked[unit][:],
@@ -166,17 +163,20 @@ def tile_scaleddotproductattention_pa_kernel(tc, q, k, v, mask, out):
             neg_max[unit] = minus_max
 
         def exponentials(unit):
+            group, member = divmod(unit, GROUP)
+            if member == 0:
+                e_sums = groups.tile([P, GROUP], F32)
+                row_sums[group] = e_sums
             e_bf16 = work.tile([P, S], BF16)
-            e_sum = small.tile([P, 1], F32)
             nc.scalar.activation(
                 out=e_bf16[:],
                 in_=masked[unit][:],
                 func=ACT.Exp,
                 bias=neg_max[unit][:],
                 scale=1.0,
-                accum_out=e_sum[:],
+                accum_out=row_sums[group][:, member : member + 1],
             )
-            e_rows[unit], row_sum[unit] = e_bf16, e_sum
+            e_rows[unit] = e_bf16
 
         def transpose_e(unit):
             e_words = e_rows[unit][:].bitcast(F32)
@@ -188,62 +188,64 @@ def tile_scaleddotproductattention_pa_kernel(tc, q, k, v, mask, out):
             e_t[unit] = e_words_t
 
         def regroup_e(unit):
-            grouped = work.tile([P, PASSES, P, PACK], BF16, align_bytes=64)
+            group, member = divmod(unit, GROUP)
+            if member == 0:
+                grouped = groups.tile([P, GROUP, PASSES, P, PACK], BF16, align_bytes=64)
+                e_grouped[group] = grouped
             nc.scalar.copy(
-                out=grouped[:].bitcast(F32),
+                out=e_grouped[group][:, member].bitcast(F32),
                 in_=e_t[unit][:].rearrange("p (g u) n -> p g n u", u=PAIR),
             )
-            e_grouped[unit] = grouped
 
-        def quantise_e(unit):
-            codes = work.tile([P, PASSES, P], U32, align_bytes=64, name="e_code_words")
-            scale_plane = work.tile([P, PASSES, P], U8, align_bytes=64, name="e_scale_plane")
-            nc.vector.quantize_mx(
-                out=codes[:].rearrange("p g n -> p (g n)").bitcast(FP8X4),
-                scales=scale_plane[:].rearrange("p g n -> p (g n)"),
-                in_=e_grouped[unit][:].rearrange("p g n t -> p (g n t)"),
+        def multiply_e_v(group):
+            head = group * GROUP // Q_TILES
+            codes = groups.tile([P, GROUP, PASSES, P], U32, align_bytes=64, name="e_code_words")
+            scale_plane = groups.tile(
+                [P, GROUP, PASSES, P], U8, align_bytes=64, name="e_scale_plane"
             )
-            e_codes[unit], e_scales[unit] = codes, scale_plane
+            nc.vector.quantize_mx(
+                out=codes[:].rearrange("p m g n -> p (m g n)").bitcast(FP8X4),
+                scales=scale_plane[:].rearrange("p m g n -> p (m g n)"),
+                in_=e_grouped[group][:].rearrange("p m g n t -> p (m g n t)"),
+            )
+            pv_bank = out_psum.tile([P, GROUP, D], F32)
+            for member in range(GROUP):
+                for g in range(PASSES):
+                    nc.tensor.matmul_mx(
+                        out=pv_bank[:, member, :],
+                        lhsT=codes[:, member, g, :].bitcast(FP8X4),
+                        lhsT_scale=scale_plane[:, member, g, :],
+                        rhs=v_codes[head][:, g, :].bitcast(FP8X4),
+                        rhs_scale=v_scales[head][:, g, :],
+                        start=(g == 0),
+                        stop=(g == PASSES - 1),
+                    )
+            pv[group] = pv_bank
+            inverse = groups.tile([P, GROUP], F32)
+            nc.vector.reciprocal(out=inverse[:], in_=row_sums[group][:])
+            row_sums[group] = inverse
 
-        def multiply_e_v(unit):
-            head = unit // Q_TILES
-            pv_bank = out_psum.tile([P, D], F32)
-            for g in range(PASSES):
-                nc.tensor.matmul_mx(
-                    out=pv_bank[:],
-                    lhsT=e_codes[unit][:, g, :].bitcast(FP8X4),
-                    lhsT_scale=e_scales[unit][:, g, :],
-                    rhs=v_codes[head][:, g, :].bitcast(FP8X4),
-                    rhs_scale=v_scales[head][:, g, :],
-                    start=(g == 0),
-                    stop=(g == PASSES - 1),
-                )
-            pv[unit] = pv_bank
-
-        def invert_row_sum(unit):
-            inverse = small.tile([P, 1], F32)
-            nc.vector.reciprocal(out=inverse[:], in_=row_sum[unit][:])
-            row_sum[unit] = inverse
-
-        def divide_and_store(unit):
-            head, tile_index = divmod(unit, Q_TILES)
-            if tile_index == 0:
+        def divide_and_store(group):
+            first_unit = group * GROUP
+            head = first_unit // Q_TILES
+            if first_unit % Q_TILES == 0:
                 out_sb = heads.tile([P, Q_TILES, D], F32)
                 out_rows[head] = out_sb
-            nc.scalar.activation(
-                out=out_rows[head][:, tile_index, :],
-                in_=pv[unit][:],
-                func=ACT.Copy,
-                scale=row_sum[unit][:],
-            )
-            if tile_index == Q_TILES - 1:
+            for member in range(GROUP):
+                nc.scalar.activation(
+                    out=out_rows[head][:, (first_unit + member) % Q_TILES, :],
+                    in_=pv[group][:, member, :],
+                    func=ACT.Copy,
+                    scale=row_sums[group][:, member : member + 1],
+                )
+            if (first_unit + GROUP) % Q_TILES == 0:
                 nc.sync.dma_start(out=out_heads[head], in_=out_rows[head][:])
 
         def is_unit(index):
             return 0 <= index < UNITS
 
         ctx.enter_context(tc.manual_schedule())
-        for step in range(-LOAD_LEAD, UNITS + PV_LAG):
+        for step in range(-LOAD_LEAD, UNITS + OUT_LAG):
             if is_unit(step + LOAD_LEAD) and (step + LOAD_LEAD) % Q_TILES == 0:
                 load_head((step + LOAD_LEAD) // Q_TILES)
             if 0 <= step + MASK_LEAD < Q_TILES:
@@ -252,23 +254,23 @@ def tile_scaleddotproductattention_pa_kernel(tc, q, k, v, mask, out):
             if is_unit(step - E_T_LAG):
                 transpose_e(step - E_T_LAG)
             if is_unit(step):
-                mask_scores(step)
+                mask_scores(step, FIRST_HALF)
+            if is_unit(step - EXP_LAG):
+                row_maximum(step - EXP_LAG)
+            if is_unit(step) and not takes_detour(step):
+                mask_scores(step, LAST_HALF)
             if is_unit(step + SCORE_LEAD):
                 multiply_q_k(step + SCORE_LEAD)
             if is_unit(step - EXP_LAG):
                 exponentials(step - EXP_LAG)
-            if is_unit(step + DETOUR_LEAD):
-                mask_scores_on_detour(step + DETOUR_LEAD)
-            if is_unit(step - PV_LAG):
-                invert_row_sum(step - PV_LAG)
-                quantise_e(step - PV_LAG)
-                multiply_e_v(step - PV_LAG)
+            if is_unit(step + DETOUR_LEAD) and takes_detour(step + DETOUR_LEAD):
+                mask_scores_on_detour(step + DETOUR_LEAD, LAST_HALF)
             if is_unit(step - E_T_LAG):
                 regroup_e(step - E_T_LAG)
-            if is_unit(step):
-                row_maximum(step)
-            if is_unit(step - PV_LAG):
-                divide_and_store(step - PV_LAG)
+            if is_unit(step - PV_LAG) and (step - PV_LAG) % GROUP == GROUP - 1:
+                multiply_e_v((step - PV_LAG) // GROUP)
+            if is_unit(step - OUT_LAG) and (step - OUT_LAG) % GROUP == GROUP - 1:
+                divide_and_store((step - OUT_LAG) // GROUP)
             if is_unit(step + V_LEAD) and (step + V_LEAD) % Q_TILES == 0:
                 quantise_v((step + V_LEAD) // Q_TILES)
             if is_unit(step + QK_T_LEAD):

@@ -30,18 +30,21 @@ WORD_BLOCKS = S // (PAIR * P)
 
 FLOPS = 2 * 2 * HEADS * S * S * D
 
-LOAD_LEAD = 18
-MASK_LEAD = 17
-QK_T_LEAD = 10
-V_LEAD = 3
+DETOURS = 2
+
+LOAD_LEAD = 16
+MASK_LEAD = 15
+Q_T_LEAD = 8
+K_T_LEAD = 4
+V_GROUP_LEAD = 6
+V_QUANT_LEAD = 2
 SCORE_LEAD = 2
 DETOUR_LEAD = 1
-EXP_LAG = 1
-E_T_LAG = 2
-PV_LAG = 4
-OUT_LAG = 5
-
-DETOUR_EVERY = 2
+MAX_LAG = 1
+EXP_LAG = 2
+E_T_LAG = 3
+PV_LAG = 7
+OUT_LAG = 8
 
 
 def tile_scaleddotproductattention_pa_kernel(tc, q, k, v, mask, out):
@@ -55,14 +58,13 @@ def tile_scaleddotproductattention_pa_kernel(tc, q, k, v, mask, out):
 
     with ExitStack() as ctx:
         consts = ctx.enter_context(tc.tile_pool(name="consts", bufs=1))
-        loads = ctx.enter_context(tc.tile_pool(name="loads", bufs=3))
         heads = ctx.enter_context(tc.tile_pool(name="heads", bufs=3))
-        work = ctx.enter_context(tc.tile_pool(name="work", bufs=4))
         groups = ctx.enter_context(tc.tile_pool(name="groups", bufs=3))
-        score_psum = ctx.enter_context(tc.psum_pool(name="score_psum", bufs=2 * HALVES))
-        e_t_psum = ctx.enter_context(tc.psum_pool(name="e_t_psum", bufs=2))
-        qk_t_psum = ctx.enter_context(tc.psum_pool(name="qk_t_psum", bufs=1))
-        out_psum = ctx.enter_context(tc.psum_pool(name="out_psum", bufs=1))
+        units = ctx.enter_context(tc.tile_pool(name="units", bufs=3))
+        masked_pool = ctx.enter_context(tc.tile_pool(name="masked_pool", bufs=5))
+        score_psum = ctx.enter_context(tc.psum_pool(name="score_psum", bufs=3 * HALVES))
+        e_t_psum = ctx.enter_context(tc.psum_pool(name="e_t_psum", bufs=1))
+        shared_psum = ctx.enter_context(tc.psum_pool(name="shared_psum", bufs=1))
 
         ident_bf16 = consts.tile([P, P], BF16)
         make_identity(nc, ident_bf16[:])
@@ -70,60 +72,69 @@ def tile_scaleddotproductattention_pa_kernel(tc, q, k, v, mask, out):
         make_identity(nc, ident_f32[:])
         mask_sb = consts.tile([P, Q_TILES, S], BF16)
 
-        q_rows, k_rows, v_rows = {}, {}, {}
-        qk_t, v_codes, v_scales, out_rows = {}, {}, {}, {}
+        q_rows, k_rows, v_rows, v_grouped = {}, {}, {}, {}
+        q_t, k_t, v_codes, v_scales, out_rows = {}, {}, {}, {}, {}
         e_grouped, row_sums, pv = {}, {}, {}
         scores, masked, neg_max, e_rows, e_t = {}, {}, {}, {}, {}
 
         def load_head(head):
-            q_in = loads.tile([P, Q_TILES, D], BF16)
+            q_in = heads.tile([P, Q_TILES, D], BF16)
             nc.sync.dma_start(out=q_in[:], in_=q_heads[head])
-            k_in = loads.tile([P, Q_TILES, D], BF16)
+            k_in = heads.tile([P, Q_TILES, D], BF16)
             nc.sync.dma_start(out=k_in[:], in_=k_heads[head])
-            v_in = loads.tile([P, PASSES, PACK, D], BF16)
+            v_in = heads.tile([P, PASSES, PACK, D], BF16)
             nc.sync.dma_start(
                 out=v_in[:].rearrange("p g (u e) d -> p (g u) (e d)", e=PAIR), in_=v_heads[head]
             )
             q_rows[head], k_rows[head], v_rows[head] = q_in, k_in, v_in
 
-        def transpose_q_and_k(unit):
-            head, tile_index = divmod(unit, Q_TILES)
-            if tile_index == 0:
-                qk_cols = heads.tile([P, 2, Q_TILES, P], BF16)
-                qk_t[head] = qk_cols
-            qk_bank = qk_t_psum.tile([P, 2, P], BF16)
-            nc.tensor.transpose(qk_bank[:, 0, :], q_rows[head][:, tile_index, :], ident_bf16[:])
-            nc.tensor.transpose(qk_bank[:, 1, :], k_rows[head][:, tile_index, :], ident_bf16[:])
-            nc.scalar.copy(out=qk_t[head][:, :, tile_index, :], in_=qk_bank[:])
+        def transpose_rows(rows):
+            t_bank = shared_psum.tile([P, Q_TILES, P], BF16, tag="shared_bank")
+            for tile_index in range(Q_TILES):
+                nc.tensor.transpose(t_bank[:, tile_index, :], rows[:, tile_index, :], ident_bf16[:])
+            return t_bank
+
+        def transpose_q(head):
+            q_cols = heads.tile([P, Q_TILES, P], BF16)
+            nc.scalar.copy(out=q_cols[:], in_=transpose_rows(q_rows[head])[:])
+            q_t[head] = q_cols
+
+        def transpose_k(head):
+            k_cols = heads.tile([P, Q_TILES, P], BF16)
+            nc.scalar.copy(out=k_cols[:], in_=transpose_rows(k_rows[head])[:])
+            k_t[head] = k_cols
+
+        def regroup_v(head):
+            grouped = heads.tile([P, PASSES, D, PACK], BF16, align_bytes=64, name="v_grouped_keys")
+            nc.vector.tensor_copy(
+                out=grouped[:], in_=v_rows[head][:].rearrange("p g t d -> p g d t")
+            )
+            v_grouped[head] = grouped
 
         def quantise_v(head):
-            v_grouped = heads.tile([P, PASSES, D, PACK], BF16, align_bytes=64)
-            nc.vector.tensor_copy(
-                out=v_grouped[:], in_=v_rows[head][:].rearrange("p g t d -> p g d t")
-            )
             codes = heads.tile([P, PASSES, D], U32, align_bytes=64, name="v_code_words")
             scale_plane = heads.tile([P, PASSES, D], U8, align_bytes=64, name="v_scale_plane")
             nc.vector.quantize_mx(
                 out=codes[:].rearrange("p g d -> p (g d)").bitcast(FP8X4),
                 scales=scale_plane[:].rearrange("p g d -> p (g d)"),
-                in_=v_grouped[:].rearrange("p g d t -> p (g d t)"),
+                in_=v_grouped[head][:].rearrange("p g d t -> p (g d t)"),
             )
             v_codes[head], v_scales[head] = codes, scale_plane
 
         def takes_detour(unit):
-            return unit % DETOUR_EVERY == 0
+            return unit % GROUP < DETOURS
 
         def multiply_q_k(unit):
             head, tile_index = divmod(unit, Q_TILES)
-            masked_rows = work.tile([P, S], F32)
+            masked_rows = masked_pool.tile([P, S], F32)
             masked[unit] = masked_rows
             for half in range(HALVES):
                 score_bank = score_psum.tile([P, BANK], F32)
                 key_tiles = slice(half * BANK // P, (half + 1) * BANK // P)
                 nc.tensor.matmul(
                     out=score_bank[:],
-                    lhsT=qk_t[head][:, 0, tile_index, :],
-                    rhs=qk_t[head][:, 1, key_tiles, :].rearrange("d t p -> d (t p)"),
+                    lhsT=q_t[head][:, tile_index, :],
+                    rhs=k_t[head][:, key_tiles, :].rearrange("d t p -> d (t p)"),
                     start=True,
                     stop=True,
                 )
@@ -142,7 +153,7 @@ def tile_scaleddotproductattention_pa_kernel(tc, q, k, v, mask, out):
 
         def mask_scores_on_detour(unit, half):
             keys = slice(half * BANK, (half + 1) * BANK)
-            scaled = work.tile([P, BANK], F32)
+            scaled = units.tile([P, BANK], F32)
             nc.scalar.mul(out=scaled[:], in_=scores[unit, half][:], mul=1.0 / TEMPERATURE)
             nc.gpsimd.tensor_tensor(
                 out=masked[unit][:, keys],
@@ -152,7 +163,7 @@ def tile_scaleddotproductattention_pa_kernel(tc, q, k, v, mask, out):
             )
 
         def row_maximum(unit):
-            minus_max = work.tile([P, 1], F32)
+            minus_max = units.tile([P, 1], F32)
             nc.vector.tensor_reduce(
                 out=minus_max[:],
                 in_=masked[unit][:],
@@ -167,7 +178,7 @@ def tile_scaleddotproductattention_pa_kernel(tc, q, k, v, mask, out):
             if member == 0:
                 e_sums = groups.tile([P, GROUP], F32)
                 row_sums[group] = e_sums
-            e_bf16 = work.tile([P, S], BF16)
+            e_bf16 = units.tile([P, S], BF16)
             nc.scalar.activation(
                 out=e_bf16[:],
                 in_=masked[unit][:],
@@ -208,7 +219,7 @@ def tile_scaleddotproductattention_pa_kernel(tc, q, k, v, mask, out):
                 scales=scale_plane[:].rearrange("p m g n -> p (m g n)"),
                 in_=e_grouped[group][:].rearrange("p m g n t -> p (m g n t)"),
             )
-            pv_bank = out_psum.tile([P, GROUP, D], F32)
+            pv_bank = shared_psum.tile([P, GROUP, D], F32, tag="shared_bank")
             for member in range(GROUP):
                 for g in range(PASSES):
                     nc.tensor.matmul_mx(
@@ -244,34 +255,47 @@ def tile_scaleddotproductattention_pa_kernel(tc, q, k, v, mask, out):
         def is_unit(index):
             return 0 <= index < UNITS
 
+        def starts_head(index):
+            return is_unit(index) and index % Q_TILES == 0
+
+        def ends_group(index):
+            return is_unit(index) and index % GROUP == GROUP - 1
+
         ctx.enter_context(tc.manual_schedule())
         for step in range(-LOAD_LEAD, UNITS + OUT_LAG):
-            if is_unit(step + LOAD_LEAD) and (step + LOAD_LEAD) % Q_TILES == 0:
+            if starts_head(step + LOAD_LEAD):
                 load_head((step + LOAD_LEAD) // Q_TILES)
             if 0 <= step + MASK_LEAD < Q_TILES:
                 tile_index = step + MASK_LEAD
                 nc.sync.dma_start(out=mask_sb[:, tile_index, :], in_=mask_tiles[0, :, tile_index, :])
+
             if is_unit(step - E_T_LAG):
                 transpose_e(step - E_T_LAG)
-            if is_unit(step):
-                mask_scores(step, FIRST_HALF)
-            if is_unit(step - EXP_LAG):
-                row_maximum(step - EXP_LAG)
-            if is_unit(step) and not takes_detour(step):
-                mask_scores(step, LAST_HALF)
             if is_unit(step + SCORE_LEAD):
                 multiply_q_k(step + SCORE_LEAD)
+
+            if is_unit(step):
+                mask_scores(step, FIRST_HALF)
+            if is_unit(step - MAX_LAG):
+                row_maximum(step - MAX_LAG)
+            if ends_group(step - PV_LAG):
+                multiply_e_v((step - PV_LAG) // GROUP)
+            if starts_head(step + V_GROUP_LEAD):
+                regroup_v((step + V_GROUP_LEAD) // Q_TILES)
+            if starts_head(step + V_QUANT_LEAD):
+                quantise_v((step + V_QUANT_LEAD) // Q_TILES)
+            if is_unit(step) and not takes_detour(step):
+                mask_scores(step, LAST_HALF)
+
             if is_unit(step - EXP_LAG):
                 exponentials(step - EXP_LAG)
             if is_unit(step + DETOUR_LEAD) and takes_detour(step + DETOUR_LEAD):
                 mask_scores_on_detour(step + DETOUR_LEAD, LAST_HALF)
             if is_unit(step - E_T_LAG):
                 regroup_e(step - E_T_LAG)
-            if is_unit(step - PV_LAG) and (step - PV_LAG) % GROUP == GROUP - 1:
-                multiply_e_v((step - PV_LAG) // GROUP)
-            if is_unit(step - OUT_LAG) and (step - OUT_LAG) % GROUP == GROUP - 1:
+            if ends_group(step - OUT_LAG):
                 divide_and_store((step - OUT_LAG) // GROUP)
-            if is_unit(step + V_LEAD) and (step + V_LEAD) % Q_TILES == 0:
-                quantise_v((step + V_LEAD) // Q_TILES)
-            if is_unit(step + QK_T_LEAD):
-                transpose_q_and_k(step + QK_T_LEAD)
+            if starts_head(step + Q_T_LEAD):
+                transpose_q((step + Q_T_LEAD) // Q_TILES)
+            if starts_head(step + K_T_LEAD):
+                transpose_k((step + K_T_LEAD) // Q_TILES)

@@ -36,7 +36,7 @@ LOAD_LEAD = 16
 MASK_LEAD = 15
 Q_T_LEAD = 8
 K_T_LEAD = 4
-V_GROUP_LEAD = 6
+V_GROUP_LEAD = 10
 V_QUANT_LEAD = 2
 SCORE_LEAD = 2
 DETOUR_LEAD = 1
@@ -73,7 +73,7 @@ def tile_scaleddotproductattention_pa_kernel(tc, q, k, v, mask, out):
         mask_sb = consts.tile([P, Q_TILES, S], BF16)
 
         q_rows, k_rows, v_rows, v_grouped = {}, {}, {}, {}
-        q_t, k_t, v_codes, v_scales, out_rows = {}, {}, {}, {}, {}
+        q_t, k_t, v_codes, v_scales = {}, {}, {}, {}
         e_grouped, row_sums, pv = {}, {}, {}
         scores, masked, neg_max, e_rows, e_t = {}, {}, {}, {}, {}
 
@@ -105,9 +105,14 @@ def tile_scaleddotproductattention_pa_kernel(tc, q, k, v, mask, out):
             k_t[head] = k_cols
 
         def regroup_v(head):
-            grouped = heads.tile([P, PASSES, D, PACK], BF16, align_bytes=64, name="v_grouped_keys")
-            nc.vector.tensor_copy(
-                out=grouped[:], in_=v_rows[head][:].rearrange("p g t d -> p g d t")
+            grouped = consts.tile([P, PASSES, D, PACK], BF16, align_bytes=64, name="v_grouped_keys")
+            nc.gpsimd.tensor_scalar(
+                out=grouped[:],
+                in0=v_rows[head][:].rearrange("p g t d -> p g d t"),
+                scalar1=1.0,
+                scalar2=0.0,
+                op0=ALU.mult,
+                op1=ALU.add,
             )
             v_grouped[head] = grouped
 
@@ -237,20 +242,18 @@ def tile_scaleddotproductattention_pa_kernel(tc, q, k, v, mask, out):
             row_sums[group] = inverse
 
         def divide_and_store(group):
-            first_unit = group * GROUP
-            head = first_unit // Q_TILES
-            if first_unit % Q_TILES == 0:
-                out_sb = heads.tile([P, Q_TILES, D], F32)
-                out_rows[head] = out_sb
+            head, first_tile = divmod(group * GROUP, Q_TILES)
+            out_sb = groups.tile([P, GROUP, D], F32)
             for member in range(GROUP):
                 nc.scalar.activation(
-                    out=out_rows[head][:, (first_unit + member) % Q_TILES, :],
+                    out=out_sb[:, member, :],
                     in_=pv[group][:, member, :],
                     func=ACT.Copy,
                     scale=row_sums[group][:, member : member + 1],
                 )
-            if (first_unit + GROUP) % Q_TILES == 0:
-                nc.sync.dma_start(out=out_heads[head], in_=out_rows[head][:])
+            nc.sync.dma_start(
+                out=out_heads[head][:, first_tile : first_tile + GROUP, :], in_=out_sb[:]
+            )
 
         def is_unit(index):
             return 0 <= index < UNITS
@@ -280,10 +283,10 @@ def tile_scaleddotproductattention_pa_kernel(tc, q, k, v, mask, out):
                 row_maximum(step - MAX_LAG)
             if ends_group(step - PV_LAG):
                 multiply_e_v((step - PV_LAG) // GROUP)
-            if starts_head(step + V_GROUP_LEAD):
-                regroup_v((step + V_GROUP_LEAD) // Q_TILES)
             if starts_head(step + V_QUANT_LEAD):
                 quantise_v((step + V_QUANT_LEAD) // Q_TILES)
+            if starts_head(step + V_GROUP_LEAD):
+                regroup_v((step + V_GROUP_LEAD) // Q_TILES)
             if is_unit(step) and not takes_detour(step):
                 mask_scores(step, LAST_HALF)
 

from contextlib import ExitStack

import concourse.mybir as mybir
from concourse.masks import make_identity

BF16 = mybir.dt.bfloat16
F32 = mybir.dt.float32
U32 = mybir.dt.uint32
U8 = mybir.dt.uint8
FP8X4 = mybir.dt.float8_e4m3fn_x4
ALU = mybir.AluOpType
ACT = mybir.ActivationFunctionType

P = 128
HEADS = 16
S = 1024
D = 128
TEMPERATURE = 8.0
Q_TILES = S // P
UNITS = HEADS * Q_TILES
GROUP = 4
BANK = 512
HALVES = S // BANK
FIRST_HALF, LAST_HALF = 0, HALVES - 1
PACK = 4
K_PASS = P * PACK
PASSES = S // K_PASS
PAIR = 2
WORD_BLOCKS = S // (PAIR * P)

FLOPS = 2 * 2 * HEADS * S * S * D

DETOURS = 2

LOAD_LEAD = 16
MASK_LEAD = 15
Q_T_LEAD = 8
K_T_LEAD = 4
V_GROUP_LEAD = 10
V_QUANT_LEAD = 2
SCORE_LEAD = 2
DETOUR_LEAD = 1
MAX_LAG = 1
EXP_LAG = 2
E_T_LAG = 3
PV_LAG = 7
OUT_LAG = 8


def tile_scaleddotproductattention_pa_kernel(tc, q, k, v, mask, out):
    nc = tc.nc

    q_heads = q.rearrange("b h (p t) d -> (b h) p t d", t=Q_TILES)
    k_heads = k.rearrange("b h (t p) d -> (b h) p t d", p=P)
    mask_tiles = mask.rearrange("a b (p t) k -> (a b) p t k", t=Q_TILES)
    out_heads = out.rearrange("b h (p t) d -> (b h) p t d", t=Q_TILES)
    v_heads = v.rearrange("b h (c p e) d -> (b h) p c (e d)", p=P, e=PAIR)

    with ExitStack() as ctx:
        consts = ctx.enter_context(tc.tile_pool(name="consts", bufs=1))
        heads = ctx.enter_context(tc.tile_pool(name="heads", bufs=3))
        groups = ctx.enter_context(tc.tile_pool(name="groups", bufs=3))
        units = ctx.enter_context(tc.tile_pool(name="units", bufs=3))
        masked_pool = ctx.enter_context(tc.tile_pool(name="masked_pool", bufs=5))
        score_psum = ctx.enter_context(tc.psum_pool(name="score_psum", bufs=3 * HALVES))
        e_t_psum = ctx.enter_context(tc.psum_pool(name="e_t_psum", bufs=1))
        shared_psum = ctx.enter_context(tc.psum_pool(name="shared_psum", bufs=1))

        ident_bf16 = consts.tile([P, P], BF16)
        make_identity(nc, ident_bf16[:])
        ident_f32 = consts.tile([P, P], F32)
        make_identity(nc, ident_f32[:])
        mask_sb = consts.tile([P, Q_TILES, S], BF16)

        q_rows, k_rows, v_rows, v_grouped = {}, {}, {}, {}
        q_t, k_t, v_codes, v_scales = {}, {}, {}, {}
        e_grouped, row_sums, pv = {}, {}, {}
        scores, masked, neg_max, e_rows, e_t = {}, {}, {}, {}, {}

        def load_head(head):
            q_in = heads.tile([P, Q_TILES, D], BF16)
            nc.sync.dma_start(out=q_in[:], in_=q_heads[head])
            k_in = heads.tile([P, Q_TILES, D], BF16)
            nc.sync.dma_start(out=k_in[:], in_=k_heads[head])
            v_in = heads.tile([P, PASSES, PACK, D], BF16)
            nc.sync.dma_start(
                out=v_in[:].rearrange("p g (u e) d -> p (g u) (e d)", e=PAIR), in_=v_heads[head]
            )
            q_rows[head], k_rows[head], v_rows[head] = q_in, k_in, v_in

        def transpose_rows(rows):
            t_bank = shared_psum.tile([P, Q_TILES, P], BF16, tag="shared_bank")
            for tile_index in range(Q_TILES):
                nc.tensor.transpose(t_bank[:, tile_index, :], rows[:, tile_index, :], ident_bf16[:])
            return t_bank

        def transpose_q(head):
            q_cols = heads.tile([P, Q_TILES, P], BF16)
            nc.scalar.copy(out=q_cols[:], in_=transpose_rows(q_rows[head])[:])
            q_t[head] = q_cols

        def transpose_k(head):
            k_cols = heads.tile([P, Q_TILES, P], BF16)
            nc.scalar.copy(out=k_cols[:], in_=transpose_rows(k_rows[head])[:])
            k_t[head] = k_cols

        def regroup_v(head):
            grouped = consts.tile([P, PASSES, D, PACK], BF16, align_bytes=64, name="v_grouped_keys")
            nc.gpsimd.tensor_scalar(
                out=grouped[:],
                in0=v_rows[head][:].rearrange("p g t d -> p g d t"),
                scalar1=1.0,
                scalar2=0.0,
                op0=ALU.mult,
                op1=ALU.add,
            )
            v_grouped[head] = grouped

        def quantise_v(head):
            codes = heads.tile([P, PASSES, D], U32, align_bytes=64, name="v_code_words")
            scale_plane = heads.tile([P, PASSES, D], U8, align_bytes=64, name="v_scale_plane")
            nc.vector.quantize_mx(
                out=codes[:].rearrange("p g d -> p (g d)").bitcast(FP8X4),
                scales=scale_plane[:].rearrange("p g d -> p (g d)"),
                in_=v_grouped[head][:].rearrange("p g d t -> p (g d t)"),
            )
            v_codes[head], v_scales[head] = codes, scale_plane

        def takes_detour(unit):
            return unit % GROUP < DETOURS

        def multiply_q_k(unit):
            head, tile_index = divmod(unit, Q_TILES)
            masked_rows = masked_pool.tile([P, S], F32)
            masked[unit] = masked_rows
            for half in range(HALVES):
                score_bank = score_psum.tile([P, BANK], F32)
                key_tiles = slice(half * BANK // P, (half + 1) * BANK // P)
                nc.tensor.matmul(
                    out=score_bank[:],
                    lhsT=q_t[head][:, tile_index, :],
                    rhs=k_t[head][:, key_tiles, :].rearrange("d t p -> d (t p)"),
                    start=True,
                    stop=True,
                )
                scores[unit, half] = score_bank

        def mask_scores(unit, half):
            keys = slice(half * BANK, (half + 1) * BANK)
            nc.vector.scalar_tensor_tensor(
                out=masked[unit][:, keys],
                in0=scores[unit, half][:],
                scalar=1.0 / TEMPERATURE,
                in1=mask_sb[:, unit % Q_TILES, keys],
                op0=ALU.mult,
                op1=ALU.mult,
            )

        def mask_scores_on_detour(unit, half):
            keys = slice(half * BANK, (half + 1) * BANK)
            scaled = units.tile([P, BANK], F32)
            nc.scalar.mul(out=scaled[:], in_=scores[unit, half][:], mul=1.0 / TEMPERATURE)
            nc.gpsimd.tensor_tensor(
                out=masked[unit][:, keys],
                in0=scaled[:],
                in1=mask_sb[:, unit % Q_TILES, keys],
                op=ALU.mult,
            )

        def row_maximum(unit):
            minus_max = units.tile([P, 1], F32)
            nc.vector.tensor_reduce(
                out=minus_max[:],
                in_=masked[unit][:],
                axis=mybir.AxisListType.X,
                op=ALU.max,
                negate=True,
            )
            neg_max[unit] = minus_max

        def exponentials(unit):
            group, member = divmod(unit, GROUP)
            if member == 0:
                e_sums = groups.tile([P, GROUP], F32)
                row_sums[group] = e_sums
            e_bf16 = units.tile([P, S], BF16)
            nc.scalar.activation(
                out=e_bf16[:],
                in_=masked[unit][:],
                func=ACT.Exp,
                bias=neg_max[unit][:],
                scale=1.0,
                accum_out=row_sums[group][:, member : member + 1],
            )
            e_rows[unit] = e_bf16

        def transpose_e(unit):
            e_words = e_rows[unit][:].bitcast(F32)
            e_words_t = e_t_psum.tile([P, WORD_BLOCKS, P], F32)
            for c in range(WORD_BLOCKS):
                nc.tensor.transpose(
                    e_words_t[:, c, :], e_words[:, c * P : (c + 1) * P], ident_f32[:]
                )
            e_t[unit] = e_words_t

        def regroup_e(unit):
            group, member = divmod(unit, GROUP)
            if member == 0:
                grouped = groups.tile([P, GROUP, PASSES, P, PACK], BF16, align_bytes=64)
                e_grouped[group] = grouped
            nc.scalar.copy(
                out=e_grouped[group][:, member].bitcast(F32),
                in_=e_t[unit][:].rearrange("p (g u) n -> p g n u", u=PAIR),
            )

        def multiply_e_v(group):
            head = group * GROUP // Q_TILES
            codes = groups.tile([P, GROUP, PASSES, P], U32, align_bytes=64, name="e_code_words")
            scale_plane = groups.tile(
                [P, GROUP, PASSES, P], U8, align_bytes=64, name="e_scale_plane"
            )
            nc.vector.quantize_mx(
                out=codes[:].rearrange("p m g n -> p (m g n)").bitcast(FP8X4),
                scales=scale_plane[:].rearrange("p m g n -> p (m g n)"),
                in_=e_grouped[group][:].rearrange("p m g n t -> p (m g n t)"),
            )
            pv_bank = shared_psum.tile([P, GROUP, D], F32, tag="shared_bank")
            for member in range(GROUP):
                for g in range(PASSES):
                    nc.tensor.matmul_mx(
                        out=pv_bank[:, member, :],
                        lhsT=codes[:, member, g, :].bitcast(FP8X4),
                        lhsT_scale=scale_plane[:, member, g, :],
                        rhs=v_codes[head][:, g, :].bitcast(FP8X4),
                        rhs_scale=v_scales[head][:, g, :],
                        start=(g == 0),
                        stop=(g == PASSES - 1),
                    )
            pv[group] = pv_bank
            inverse = groups.tile([P, GROUP], F32)
            nc.vector.reciprocal(out=inverse[:], in_=row_sums[group][:])
            row_sums[group] = inverse

        def divide_and_store(group):
            head, first_tile = divmod(group * GROUP, Q_TILES)
            out_sb = groups.tile([P, GROUP, D], F32)
            for member in range(GROUP):
                nc.scalar.activation(
                    out=out_sb[:, member, :],
                    in_=pv[group][:, member, :],
                    func=ACT.Copy,
                    scale=row_sums[group][:, member : member + 1],
                )
            nc.sync.dma_start(
                out=out_heads[head][:, first_tile : first_tile + GROUP, :], in_=out_sb[:]
            )

        def is_unit(index):
            return 0 <= index < UNITS

        def starts_head(index):
            return is_unit(index) and index % Q_TILES == 0

        def ends_group(index):
            return is_unit(index) and index % GROUP == GROUP - 1

        ctx.enter_context(tc.manual_schedule())
        for step in range(-LOAD_LEAD, UNITS + OUT_LAG):
            if starts_head(step + LOAD_LEAD):
                load_head((step + LOAD_LEAD) // Q_TILES)
            if 0 <= step + MASK_LEAD < Q_TILES:
                tile_index = step + MASK_LEAD
                nc.sync.dma_start(out=mask_sb[:, tile_index, :], in_=mask_tiles[0, :, tile_index, :])

            if is_unit(step - E_T_LAG):
                transpose_e(step - E_T_LAG)
            if is_unit(step + SCORE_LEAD):
                multiply_q_k(step + SCORE_LEAD)

            if is_unit(step):
                mask_scores(step, FIRST_HALF)
            if is_unit(step - MAX_LAG):
                row_maximum(step - MAX_LAG)
            if ends_group(step - PV_LAG):
                multiply_e_v((step - PV_LAG) // GROUP)
            if starts_head(step + V_QUANT_LEAD):
                quantise_v((step + V_QUANT_LEAD) // Q_TILES)
            if starts_head(step + V_GROUP_LEAD):
                regroup_v((step + V_GROUP_LEAD) // Q_TILES)
            if is_unit(step) and not takes_detour(step):
                mask_scores(step, LAST_HALF)

            if is_unit(step - EXP_LAG):
                exponentials(step - EXP_LAG)
            if is_unit(step + DETOUR_LEAD) and takes_detour(step + DETOUR_LEAD):
                mask_scores_on_detour(step + DETOUR_LEAD, LAST_HALF)
            if is_unit(step - E_T_LAG):
                regroup_e(step - E_T_LAG)
            if ends_group(step - OUT_LAG):
                divide_and_store((step - OUT_LAG) // GROUP)
            if starts_head(step + Q_T_LEAD):
                transpose_q((step + Q_T_LEAD) // Q_TILES)
            if starts_head(step + K_T_LEAD):
                transpose_k((step + K_T_LEAD) // Q_TILES)
